import numpy as np
import ml_dtypes


def mxq(x, axis, fmt="e4m3"):
    dtype, down = {"e4m3": (ml_dtypes.float8_e4m3fn, 7), "e5m2": (ml_dtypes.float8_e5m2, 14)}[fmt]
    v = np.moveaxis(np.asarray(x, np.float32).astype(ml_dtypes.bfloat16).astype(np.float64), axis, -1)
    blocks = v.reshape(v.shape[:-1] + (-1, 32))
    amax = np.abs(blocks).max(-1, keepdims=True)
    byte = np.maximum(np.where(amax > 0, np.frexp(amax)[1] - 1 + 127, 0) - down, 1)
    scale = np.exp2(byte - 127.0)
    codes = (blocks / scale).astype(np.float32).astype(dtype).astype(np.float64)
    return np.moveaxis((codes * scale).reshape(v.shape), -1, axis)


WIDE = False


def mx_kscale(k):
    if not WIDE:
        return np.ones(k)
    levels = np.array([10, -10, 5, -5, 0])
    a = np.random.permutation(np.resize(levels, k // 512 * 4)).reshape(k // 512, 4)
    idx = np.arange(k)
    return np.exp2(a[idx // 512, idx % 128 // 32])


BF16 = ml_dtypes.bfloat16


def bf(x):
    return np.asarray(x, np.float32).astype(BF16)


def f64(x):
    return np.asarray(x).astype(np.float64)


B, I, H, L, P, G = 4096, 1024, 256, 4, 2, 4


def sigmoid(v):
    return 1.0 / (1.0 + np.exp(-v))


def setup_inputs():
    s = mx_kscale(I)
    return {"h_below": bf(np.random.standard_normal((B, I)) * 0.3 * s),
            "gates_rec": bf(np.random.standard_normal((B, G * H)) * 0.7),
            "c": bf(np.random.standard_normal((B, H))),
            "w_ih": bf(np.random.standard_normal((G * H, I)) * 1.5 / np.sqrt(I) / s),
            "b_ih": bf(np.random.standard_normal(G * H) * 0.3),
            "b_hh": bf(np.random.standard_normal(G * H) * 0.3)}


def reference(h_below, gates_rec, c, w_ih, b_ih, b_hh):
    gates = (mxq(f64(h_below), 1, "e4m3") @ mxq(f64(w_ih), 1, "e4m3").T) + f64(b_ih) + f64(gates_rec) + f64(b_hh)
    i, f, g, o = np.split(gates, G, axis=-1)
    c_new = sigmoid(f) * f64(c) + sigmoid(i) * np.tanh(g)
    h_new = sigmoid(o) * np.tanh(c_new)
    return h_new, c_new

@@ -1,0 +1,240 @@
+from contextlib import ExitStack
+
+import concourse.mybir as mybir
+from concourse.masks import make_identity
+
+FLOPS = 2 * 4096 * 1024 * 1024
+
+F32 = mybir.dt.float32
+BF16 = mybir.dt.bfloat16
+U32 = mybir.dt.uint32
+U8 = mybir.dt.uint8
+FP8X4 = mybir.dt.float8_e4m3fn_x4
+ACT = mybir.ActivationFunctionType
+ALU = mybir.AluOpType
+
+P = 128
+B = 4096
+K = 1024
+N = 1024
+H = 256
+NT = B // P
+GT = 4
+NG = NT // GT
+NPAIR = NT // 2
+POOL_GROUPS = 7
+
+
+def tile_yourlstm_pc_t_kernel(tc, h_below, gates_rec, c, w_ih, b_ih, b_hh, out_0, out_1):
+    nc = tc.nc
+    h_v = h_below.rearrange("(p t) k -> p (t k)", t=NT)
+    r_v = gates_rec.rearrange("(p t) n -> p (t n)", t=NT)
+    c_v = c.rearrange("(p t) n -> p (t n)", t=NT)
+    oh_v = out_0.rearrange("(p t) n -> p (t n)", t=NT)
+    oc_v = out_1.rearrange("(p t) n -> p (t n)", t=NT)
+    w_v = w_ih.rearrange("(a p) k -> p a k", p=P)
+
+    with ExitStack() as ctx:
+        const = ctx.enter_context(tc.tile_pool(name="const", bufs=1))
+        loads = ctx.enter_context(tc.tile_pool(name="loads", bufs=3))
+        work = ctx.enter_context(tc.tile_pool(name="work", bufs=3))
+        psum = ctx.enter_context(tc.psum_pool(name="psum", bufs=1))
+
+        h_t = {}
+        r_t = {}
+        c_t = {}
+        x_t = {}
+        cn_t = {}
+        hn_t = {}
+        tp_t = {}
+        gq_t = {}
+        hc_t = {}
+        hs_t = {}
+
+        def load_rec(j):
+            q = j // 2
+            if j % 2 == 0:
+                r_t[q] = loads.tile([P, GT * N], BF16, tag="rec", name="rec_sb")
+            lo = (j % 2) * 2 * N
+            nc.sync.dma_start(out=r_t[q][:, lo:lo + 2 * N], in_=r_v[:, j * 2 * N:(j + 1) * 2 * N])
+
+        def load_h(j):
+            q = j // 2
+            if j % 2 == 0:
+                h_t[q] = loads.tile([P, GT * K], BF16, tag="h", name="h_sb")
+            lo = (j % 2) * 2 * K
+            nc.sync.dma_start(out=h_t[q][:, lo:lo + 2 * K], in_=h_v[:, j * 2 * K:(j + 1) * 2 * K])
+
+        def load_c(q):
+            c_t[q] = loads.tile([P, GT * H], BF16, tag="c", bufs=4, name="c_sb")
+            nc.sync.dma_start(out=c_t[q][:], in_=c_v[:, q * GT * H:(q + 1) * GT * H])
+
+        ident = const.tile([P, P], F32, name="ident")
+        make_identity(nc, ident[:])
+        ones = const.tile([P, P], BF16, name="ones")
+        nc.vector.memset(ones[:], 1.0)
+        brow = const.tile([P, N], BF16, name="brow")
+        nc.vector.memset(brow[:], 0.0)
+        nc.sync.dma_start(out=brow[0:1, :], in_=b_ih.rearrange("(o n) -> o n", o=1))
+        nc.sync.dma_start(out=brow[1:2, :], in_=b_hh.rearrange("(o n) -> o n", o=1))
+        warm = const.tile([P, 1], F32, name="warm")
+        nc.vector.memset(warm[:], 0.0)
+        nc.scalar.activation(out=warm[:], in_=warm[:], func=ACT.Sigmoid)
+
+        load_rec(0)
+        w_sb = const.tile([P, 8 * K], BF16, name="w_sb")
+        w_sb3 = w_sb[:].rearrange("p (a k) -> p a k", a=8)
+        for i in range(4):
+            nc.sync.dma_start(out=w_sb3[:, 2 * i:2 * i + 2, :], in_=w_v[:, 2 * i:2 * i + 2, :])
+        load_h(0)
+        load_rec(1)
+        load_h(1)
+        load_c(0)
+
+        bias_ps = [psum.tile([P, 512], F32, name="bias%d" % i) for i in range(2)]
+        for i in range(2):
+            nc.tensor.matmul(bias_ps[i][:], lhsT=ones[:], rhs=brow[:, 512 * i:512 * (i + 1)], start=True, stop=True)
+
+        w_words = w_sb[:].bitcast(F32)
+        wq = const.tile([P, 2 * N * 4], BF16, name="wq", align_bytes=64)
+        wq_w = wq[:].bitcast(F32).rearrange("p (g n u) -> p g n u", g=2, u=2)
+        wc = const.tile([P, 2 * N], U32, name="wc", align_bytes=64)
+        ws = const.tile([P, 2 * N], U8, name="ws", align_bytes=64)
+        for a in range(8):
+            wtp = psum.tile([P, 512], F32, tag="acc", bufs=4, name="wtp")
+            for jj in range(4):
+                nc.tensor.transpose(
+                    wtp[:, P * jj:P * (jj + 1)],
+                    w_words[:, 512 * a + P * jj:512 * a + P * (jj + 1)],
+                    ident[:],
+                )
+            src = wtp[:].rearrange("p (g u r) -> p g r u", g=2, u=2)
+            dst = wq_w[:, :, P * a:P * (a + 1), :]
+            if a % 2 == 0:
+                nc.vector.tensor_copy(out=dst, in_=src)
+            else:
+                nc.scalar.copy(out=dst, in_=src)
+            if a % 4 == 3:
+                nh = a // 4
+                for g in range(2):
+                    lo = g * N + nh * 512
+                    nc.vector.quantize_mx(
+                        out=wc[:, lo:lo + 512].bitcast(FP8X4),
+                        scales=ws[:, lo:lo + 512],
+                        in_=wq[:, lo * 4:(lo + 512) * 4],
+                    )
+
+        def transposes(j):
+            q = j // 2
+            words = h_t[q][:].bitcast(F32)
+            gq = work.tile([P, 2 * K], BF16, tag="gq", name="gq", align_bytes=64)
+            gq_t[j] = gq
+            gq_w = gq[:].bitcast(F32).rearrange("p (a g r u) -> p a g r u", a=2, g=2, u=2)
+            for a in range(2):
+                tl = (j % 2) * 2 + a
+                tp = psum.tile([P, 512], F32, tag="tp", bufs=2, name="tp")
+                for jj in range(4):
+                    nc.tensor.transpose(
+                        tp[:, P * jj:P * (jj + 1)],
+                        words[:, 512 * tl + P * jj:512 * tl + P * (jj + 1)],
+                        ident[:],
+                    )
+                nc.scalar.copy(out=gq_w[:, a], in_=tp[:].rearrange("p (g u r) -> p g r u", g=2, u=2))
+
+        def quantise(j):
+            hc = work.tile([P, 512], U32, tag="hc", name="hc", align_bytes=64)
+            hs = work.tile([P, 512], U8, tag="hs", name="hs", align_bytes=64)
+            hc_t[j] = hc
+            hs_t[j] = hs
+            nc.vector.quantize_mx(out=hc[:].bitcast(FP8X4), scales=hs[:], in_=gq_t[j][:])
+
+        def add_bias(j):
+            q = j // 2
+            if j % 2 == 0:
+                x_t[q] = work.tile([P, GT * N], F32, tag="x", name="x_sb")
+            x3 = x_t[q][:].rearrange("p (a n) -> p a n", a=GT)
+            r3 = r_t[q][:].rearrange("p (a n) -> p a n", a=GT)
+            a0 = (j % 2) * 2
+            for i in range(2):
+                nc.vector.tensor_tensor(
+                    out=x3[:, a0:a0 + 2, 512 * i:512 * (i + 1)],
+                    in0=bias_ps[i][:].unsqueeze(1).to_broadcast([P, 2, 512]),
+                    in1=r3[:, a0:a0 + 2, 512 * i:512 * (i + 1)],
+                    op=ALU.add,
+                )
+
+        def project(j):
+            q = j // 2
+            x3 = x_t[q][:].rearrange("p (a n) -> p a n", a=GT)
+            for a in range(2):
+                tl = (j % 2) * 2 + a
+                for nh in range(2):
+                    acc = psum.tile([P, 512], F32, tag="acc", bufs=4, name="acc")
+                    for g in range(2):
+                        lo = (a * 2 + g) * P
+                        wlo = g * N + nh * 512
+                        nc.tensor.matmul_mx(
+                            out=acc[:],
+                            lhsT=hc_t[j][:, lo:lo + P].bitcast(FP8X4),
+                            lhsT_scale=hs_t[j][:, lo:lo + P],
+                            rhs=wc[:, wlo:wlo + 512].bitcast(FP8X4),
+                            rhs_scale=ws[:, wlo:wlo + 512],
+                            start=(g == 0),
+                            stop=(g == 1),
+                        )
+                    nc.vector.tensor_tensor(
+                        out=x3[:, tl, 512 * nh:512 * (nh + 1)],
+                        in0=acc[:],
+                        in1=x3[:, tl, 512 * nh:512 * (nh + 1)],
+                        op=ALU.add,
+                    )
+
+        def activate(j):
+            q = j // 2
+            x3 = x_t[q][:].rearrange("p (a n) -> p a n", a=GT)
+            a0 = (j % 2) * 2
+            nc.scalar.activation(out=x3[:, a0:a0 + 2, 0:512], in_=x3[:, a0:a0 + 2, 0:512], func=ACT.Sigmoid)
+            nc.scalar.activation(out=x3[:, a0:a0 + 2, 512:768], in_=x3[:, a0:a0 + 2, 512:768], func=ACT.Tanh)
+            nc.scalar.activation(out=x3[:, a0:a0 + 2, 768:1024], in_=x3[:, a0:a0 + 2, 768:1024], func=ACT.Sigmoid)
+
+        def cell(q, a0, na, eng):
+            if a0 == 0:
+                cn_t[q] = work.tile([P, GT * H], F32, tag="cn", name="cn_sb")
+                hn_t[q] = work.tile([P, GT * H], F32, tag="hn", name="hn_sb")
+            x3 = x_t[q][:].rearrange("p (a n) -> p a n", a=GT)
+            c3 = c_t[q][:].rearrange("p (a n) -> p a n", a=GT)
+            cn3 = cn_t[q][:].rearrange("p (a n) -> p a n", a=GT)
+            hn3 = hn_t[q][:].rearrange("p (a n) -> p a n", a=GT)
+            s = slice(a0, a0 + na)
+            eng.tensor_tensor(out=x3[:, s, 0:256], in0=x3[:, s, 0:256], in1=x3[:, s, 512:768], op=ALU.mult)
+            eng.tensor_tensor(out=x3[:, s, 256:512], in0=x3[:, s, 256:512], in1=c3[:, s, :], op=ALU.mult)
+            eng.tensor_tensor(out=cn3[:, s, :], in0=x3[:, s, 0:256], in1=x3[:, s, 256:512], op=ALU.add)
+            nc.scalar.activation(out=x3[:, s, 512:768], in_=cn3[:, s, :], func=ACT.Tanh)
+            eng.tensor_tensor(out=hn3[:, s, :], in0=x3[:, s, 768:1024], in1=x3[:, s, 512:768], op=ALU.mult)
+            lo = (q * GT + a0) * H
+            nc.sync.dma_start(out=oc_v[:, lo:lo + na * H], in_=cn_t[q][:, a0 * H:(a0 + na) * H])
+            nc.sync.dma_start(out=oh_v[:, lo:lo + na * H], in_=hn_t[q][:, a0 * H:(a0 + na) * H])
+
+        for j in range(2):
+            add_bias(j)
+            transposes(j)
+            quantise(j)
+        for j in range(NPAIR):
+            if j + 2 < NPAIR:
+                load_rec(j + 2)
+                load_h(j + 2)
+                if j % 2 == 0:
+                    load_c(j // 2 + 1)
+                transposes(j + 2)
+                add_bias(j + 2)
+            project(j)
+            if j + 2 < NPAIR:
+                quantise(j + 2)
+            activate(j)
+            q = j // 2
+            if q < POOL_GROUPS:
+                if j % 2 == 1:
+                    cell(q, 0, GT, nc.gpsimd)
+            else:
+                cell(q, (j % 2) * 2, 1, nc.vector)
+                cell(q, (j % 2) * 2 + 1, 1, nc.vector)

@@ -20,9 +20,12 @@ N = 1024
 H = 256
 NT = B // P
 GT = 4
-NG = NT // GT
 NPAIR = NT // 2
-POOL_GROUPS = 7
+LOOK = 4
+POOL_BIAS_PAIRS = (3, 4, 5)
+POOL_UNITS = ((0, 4), (4, 4), (8, 4), (12, 4), (16, 4), (20, 4), (24, 2))
+TANH_LAG = 2
+STORE_LAG = 2
 
 
 def tile_yourlstm_pc_t_kernel(tc, h_below, gates_rec, c, w_ih, b_ih, b_hh, out_0, out_1):
@@ -35,6 +38,7 @@ def tile_yourlstm_pc_t_kernel(tc, h_below, gates_rec, c, w_ih, b_ih, b_hh, out_0
     w_v = w_ih.rearrange("(a p) k -> p a k", p=P)
 
     with ExitStack() as ctx:
+        ctx.enter_context(tc.manual_schedule())
         const = ctx.enter_context(tc.tile_pool(name="const", bufs=1))
         loads = ctx.enter_context(tc.tile_pool(name="loads", bufs=3))
         work = ctx.enter_context(tc.tile_pool(name="work", bufs=3))
@@ -50,17 +54,18 @@ def tile_yourlstm_pc_t_kernel(tc, h_below, gates_rec, c, w_ih, b_ih, b_hh, out_0
         gq_t = {}
         hc_t = {}
         hs_t = {}
+        acc_t = {}
 
         def load_rec(j):
             q = j // 2
-            if j % 2 == 0:
+            if q not in r_t:
                 r_t[q] = loads.tile([P, GT * N], BF16, tag="rec", name="rec_sb")
             lo = (j % 2) * 2 * N
             nc.sync.dma_start(out=r_t[q][:, lo:lo + 2 * N], in_=r_v[:, j * 2 * N:(j + 1) * 2 * N])
 
         def load_h(j):
             q = j // 2
-            if j % 2 == 0:
+            if q not in h_t:
                 h_t[q] = loads.tile([P, GT * K], BF16, tag="h", name="h_sb")
             lo = (j % 2) * 2 * K
             nc.sync.dma_start(out=h_t[q][:, lo:lo + 2 * K], in_=h_v[:, j * 2 * K:(j + 1) * 2 * K])
@@ -68,6 +73,17 @@ def tile_yourlstm_pc_t_kernel(tc, h_below, gates_rec, c, w_ih, b_ih, b_hh, out_0
         def load_c(q):
             c_t[q] = loads.tile([P, GT * H], BF16, tag="c", bufs=4, name="c_sb")
             nc.sync.dma_start(out=c_t[q][:], in_=c_v[:, q * GT * H:(q + 1) * GT * H])
+
+        w_sb = const.tile([P, 8 * K], BF16, name="w_sb")
+        w_sb3 = w_sb[:].rearrange("p (a k) -> p a k", a=8)
+
+        def load_w(i):
+            nc.sync.dma_start(out=w_sb3[:, 2 * i:2 * i + 2, :], in_=w_v[:, 2 * i:2 * i + 2, :])
+
+        def x3(q):
+            if q not in x_t:
+                x_t[q] = work.tile([P, GT * N], F32, tag="x", bufs=5, name="x_sb")
+            return x_t[q][:].rearrange("p (a n) -> p a n", a=GT)
 
         ident = const.tile([P, P], F32, name="ident")
         make_identity(nc, ident[:])
@@ -82,19 +98,132 @@ def tile_yourlstm_pc_t_kernel(tc, h_below, gates_rec, c, w_ih, b_ih, b_hh, out_0
         nc.scalar.activation(out=warm[:], in_=warm[:], func=ACT.Sigmoid)
 
         load_rec(0)
-        w_sb = const.tile([P, 8 * K], BF16, name="w_sb")
-        w_sb3 = w_sb[:].rearrange("p (a k) -> p a k", a=8)
-        for i in range(4):
-            nc.sync.dma_start(out=w_sb3[:, 2 * i:2 * i + 2, :], in_=w_v[:, 2 * i:2 * i + 2, :])
+        load_w(0)
+        load_w(1)
+        load_rec(3)
+        load_w(2)
+        load_w(3)
         load_h(0)
         load_rec(1)
         load_h(1)
+        load_rec(2)
+        load_rec(4)
+        load_h(2)
         load_c(0)
+        load_h(3)
+        load_rec(5)
+        load_c(1)
 
         bias_ps = [psum.tile([P, 512], F32, name="bias%d" % i) for i in range(2)]
+        bias_sb = const.tile([P, N], F32, name="bias_sb")
         for i in range(2):
             nc.tensor.matmul(bias_ps[i][:], lhsT=ones[:], rhs=brow[:, 512 * i:512 * (i + 1)], start=True, stop=True)
+        for i in range(2):
+            nc.scalar.copy(out=bias_sb[:, 512 * i:512 * (i + 1)], in_=bias_ps[i][:])
 
+        def add_bias(j, i):
+            q = j // 2
+            r3 = r_t[q][:].rearrange("p (a n) -> p a n", a=GT)
+            a0 = (j % 2) * 2
+            nc.vector.tensor_tensor(
+                out=x3(q)[:, a0:a0 + 2, 512 * i:512 * (i + 1)],
+                in0=bias_ps[i][:].unsqueeze(1).to_broadcast([P, 2, 512]),
+                in1=r3[:, a0:a0 + 2, 512 * i:512 * (i + 1)],
+                op=ALU.add,
+            )
+
+        def add_bias_pool(j):
+            q = j // 2
+            r3 = r_t[q][:].rearrange("p (a n) -> p a n", a=GT)
+            a0 = (j % 2) * 2
+            nc.gpsimd.tensor_tensor(
+                out=x3(q)[:, a0:a0 + 2, :],
+                in0=r3[:, a0:a0 + 2, :],
+                in1=bias_sb[:].unsqueeze(1).to_broadcast([P, 2, N]),
+                op=ALU.add,
+            )
+
+        def transposes(j, a):
+            words = h_t[j // 2][:].bitcast(F32)
+            tl = (j % 2) * 2 + a
+            tp = psum.tile([P, 512], F32, tag="tp", bufs=2, name="tp")
+            tp_t[(j, a)] = tp
+            for jj in range(4):
+                nc.tensor.transpose(
+                    tp[:, P * jj:P * (jj + 1)],
+                    words[:, 512 * tl + P * jj:512 * tl + P * (jj + 1)],
+                    ident[:],
+                )
+
+        def regroup(j, a):
+            if a == 0:
+                gq_t[j] = work.tile([P, 2 * K], BF16, tag="gq", name="gq", align_bytes=64)
+            gq_w = gq_t[j][:].bitcast(F32).rearrange("p (a g r u) -> p a g r u", a=2, g=2, u=2)
+            nc.scalar.copy(out=gq_w[:, a], in_=tp_t[(j, a)][:].rearrange("p (g u r) -> p g r u", g=2, u=2))
+
+        def quantise(j):
+            hc_t[j] = work.tile([P, 512], U32, tag="hc", name="hc", align_bytes=64)
+            hs_t[j] = work.tile([P, 512], U8, tag="hs", name="hs", align_bytes=64)
+            nc.vector.quantize_mx(out=hc_t[j][:].bitcast(FP8X4), scales=hs_t[j][:], in_=gq_t[j][:])
+
+        def project(j, a, nh):
+            acc = psum.tile([P, 512], F32, tag="acc", bufs=4, name="acc")
+            acc_t[(j, a, nh)] = acc
+            for g in range(2):
+                lo = (a * 2 + g) * P
+                wlo = g * N + nh * 512
+                nc.tensor.matmul_mx(
+                    out=acc[:],
+                    lhsT=hc_t[j][:, lo:lo + P].bitcast(FP8X4),
+                    lhsT_scale=hs_t[j][:, lo:lo + P],
+                    rhs=wc[:, wlo:wlo + 512].bitcast(FP8X4),
+                    rhs_scale=ws[:, wlo:wlo + 512],
+                    start=(g == 0),
+                    stop=(g == 1),
+                )
+
+        def add_proj(j, a, nh):
+            tl = (j % 2) * 2 + a
+            dst = x3(j // 2)[:, tl, 512 * nh:512 * (nh + 1)]
+            nc.vector.tensor_tensor(out=dst, in0=acc_t[(j, a, nh)][:], in1=dst, op=ALU.add)
+
+        def activate(t):
+            xt = x3(t // GT)[:, t % GT, :]
+            nc.scalar.activation(out=xt[:, 0:512], in_=xt[:, 0:512], func=ACT.Sigmoid)
+            nc.scalar.activation(out=xt[:, 512:768], in_=xt[:, 512:768], func=ACT.Tanh)
+            nc.scalar.activation(out=xt[:, 768:1024], in_=xt[:, 768:1024], func=ACT.Sigmoid)
+
+        def out3(tiles, q, tag):
+            if q not in tiles:
+                tiles[q] = work.tile([P, GT * H], F32, tag=tag, name=tag + "_sb")
+            return tiles[q][:].rearrange("p (a n) -> p a n", a=GT)
+
+        def cell_state(t0, nt, eng):
+            q = t0 // GT
+            s = slice(t0 % GT, t0 % GT + nt)
+            x = x3(q)
+            c3 = c_t[q][:].rearrange("p (a n) -> p a n", a=GT)
+            eng.tensor_tensor(out=x[:, s, 0:256], in0=x[:, s, 0:256], in1=x[:, s, 512:768], op=ALU.mult)
+            eng.tensor_tensor(out=x[:, s, 256:512], in0=x[:, s, 256:512], in1=c3[:, s, :], op=ALU.mult)
+            eng.tensor_tensor(out=out3(cn_t, q, "cn")[:, s, :], in0=x[:, s, 0:256], in1=x[:, s, 256:512], op=ALU.add)
+
+        def cell_tanh(t0, nt):
+            q = t0 // GT
+            s = slice(t0 % GT, t0 % GT + nt)
+            nc.scalar.activation(out=x3(q)[:, s, 512:768], in_=out3(cn_t, q, "cn")[:, s, :], func=ACT.Tanh)
+
+        def hidden(t0, nt, eng):
+            q = t0 // GT
+            s = slice(t0 % GT, t0 % GT + nt)
+            x = x3(q)
+            eng.tensor_tensor(out=out3(hn_t, q, "hn")[:, s, :], in0=x[:, s, 768:1024], in1=x[:, s, 512:768], op=ALU.mult)
+
+        def store(dram, tiles, t0, nt):
+            lo = (t0 % GT) * H
+            nc.sync.dma_start(out=dram[:, t0 * H:(t0 + nt) * H], in_=tiles[t0 // GT][:, lo:lo + nt * H])
+
+        add_bias(0, 0)
+        add_bias(0, 1)
         w_words = w_sb[:].bitcast(F32)
         wq = const.tile([P, 2 * N * 4], BF16, name="wq", align_bytes=64)
         wq_w = wq[:].bitcast(F32).rearrange("p (g n u) -> p g n u", g=2, u=2)
@@ -110,131 +239,106 @@ def tile_yourlstm_pc_t_kernel(tc, h_below, gates_rec, c, w_ih, b_ih, b_hh, out_0
                 )
             src = wtp[:].rearrange("p (g u r) -> p g r u", g=2, u=2)
             dst = wq_w[:, :, P * a:P * (a + 1), :]
-            if a % 2 == 0:
+            if a % 2 == 1:
                 nc.vector.tensor_copy(out=dst, in_=src)
             else:
                 nc.scalar.copy(out=dst, in_=src)
             if a % 4 == 3:
-                nh = a // 4
                 for g in range(2):
-                    lo = g * N + nh * 512
+                    lo = g * N + (a // 4) * 512
                     nc.vector.quantize_mx(
                         out=wc[:, lo:lo + 512].bitcast(FP8X4),
                         scales=ws[:, lo:lo + 512],
                         in_=wq[:, lo * 4:(lo + 512) * 4],
                     )
+        for j in POOL_BIAS_PAIRS:
+            add_bias_pool(j)
+        for a in range(2):
+            transposes(0, a)
+            regroup(0, a)
+        quantise(0)
+        add_bias(1, 0)
+        add_bias(1, 1)
+        for a in range(2):
+            transposes(1, a)
+            regroup(1, a)
+        quantise(1)
 
-        def transposes(j):
-            q = j // 2
-            words = h_t[q][:].bitcast(F32)
-            gq = work.tile([P, 2 * K], BF16, tag="gq", name="gq", align_bytes=64)
-            gq_t[j] = gq
-            gq_w = gq[:].bitcast(F32).rearrange("p (a g r u) -> p a g r u", a=2, g=2, u=2)
-            for a in range(2):
-                tl = (j % 2) * 2 + a
-                tp = psum.tile([P, 512], F32, tag="tp", bufs=2, name="tp")
-                for jj in range(4):
-                    nc.tensor.transpose(
-                        tp[:, P * jj:P * (jj + 1)],
-                        words[:, 512 * tl + P * jj:512 * tl + P * (jj + 1)],
-                        ident[:],
-                    )
-                nc.scalar.copy(out=gq_w[:, a], in_=tp[:].rearrange("p (g u r) -> p g r u", g=2, u=2))
+        state_at = {}
+        tanh_at = {}
+        store_at = {}
+        pool_tiles = set()
+        for u in POOL_UNITS:
+            step = (u[0] + u[1]) // 2
+            state_at[step] = u
+            tanh_at[step + TANH_LAG] = u
+            store_at[step + TANH_LAG + STORE_LAG] = u
+            for t in range(u[0], u[0] + u[1]):
+                pool_tiles.add(t)
 
-        def quantise(j):
-            hc = work.tile([P, 512], U32, tag="hc", name="hc", align_bytes=64)
-            hs = work.tile([P, 512], U8, tag="hs", name="hs", align_bytes=64)
-            hc_t[j] = hc
-            hs_t[j] = hs
-            nc.vector.quantize_mx(out=hc[:].bitcast(FP8X4), scales=hs[:], in_=gq_t[j][:])
-
-        def add_bias(j):
-            q = j // 2
-            if j % 2 == 0:
-                x_t[q] = work.tile([P, GT * N], F32, tag="x", name="x_sb")
-            x3 = x_t[q][:].rearrange("p (a n) -> p a n", a=GT)
-            r3 = r_t[q][:].rearrange("p (a n) -> p a n", a=GT)
-            a0 = (j % 2) * 2
-            for i in range(2):
-                nc.vector.tensor_tensor(
-                    out=x3[:, a0:a0 + 2, 512 * i:512 * (i + 1)],
-                    in0=bias_ps[i][:].unsqueeze(1).to_broadcast([P, 2, 512]),
-                    in1=r3[:, a0:a0 + 2, 512 * i:512 * (i + 1)],
-                    op=ALU.add,
-                )
-
-        def project(j):
-            q = j // 2
-            x3 = x_t[q][:].rearrange("p (a n) -> p a n", a=GT)
-            for a in range(2):
-                tl = (j % 2) * 2 + a
-                for nh in range(2):
-                    acc = psum.tile([P, 512], F32, tag="acc", bufs=4, name="acc")
-                    for g in range(2):
-                        lo = (a * 2 + g) * P
-                        wlo = g * N + nh * 512
-                        nc.tensor.matmul_mx(
-                            out=acc[:],
-                            lhsT=hc_t[j][:, lo:lo + P].bitcast(FP8X4),
-                            lhsT_scale=hs_t[j][:, lo:lo + P],
-                            rhs=wc[:, wlo:wlo + 512].bitcast(FP8X4),
-                            rhs_scale=ws[:, wlo:wlo + 512],
-                            start=(g == 0),
-                            stop=(g == 1),
-                        )
-                    nc.vector.tensor_tensor(
-                        out=x3[:, tl, 512 * nh:512 * (nh + 1)],
-                        in0=acc[:],
-                        in1=x3[:, tl, 512 * nh:512 * (nh + 1)],
-                        op=ALU.add,
-                    )
-
-        def activate(j):
-            q = j // 2
-            x3 = x_t[q][:].rearrange("p (a n) -> p a n", a=GT)
-            a0 = (j % 2) * 2
-            nc.scalar.activation(out=x3[:, a0:a0 + 2, 0:512], in_=x3[:, a0:a0 + 2, 0:512], func=ACT.Sigmoid)
-            nc.scalar.activation(out=x3[:, a0:a0 + 2, 512:768], in_=x3[:, a0:a0 + 2, 512:768], func=ACT.Tanh)
-            nc.scalar.activation(out=x3[:, a0:a0 + 2, 768:1024], in_=x3[:, a0:a0 + 2, 768:1024], func=ACT.Sigmoid)
-
-        def cell(q, a0, na, eng):
-            if a0 == 0:
-                cn_t[q] = work.tile([P, GT * H], F32, tag="cn", name="cn_sb")
-                hn_t[q] = work.tile([P, GT * H], F32, tag="hn", name="hn_sb")
-            x3 = x_t[q][:].rearrange("p (a n) -> p a n", a=GT)
-            c3 = c_t[q][:].rearrange("p (a n) -> p a n", a=GT)
-            cn3 = cn_t[q][:].rearrange("p (a n) -> p a n", a=GT)
-            hn3 = hn_t[q][:].rearrange("p (a n) -> p a n", a=GT)
-            s = slice(a0, a0 + na)
-            eng.tensor_tensor(out=x3[:, s, 0:256], in0=x3[:, s, 0:256], in1=x3[:, s, 512:768], op=ALU.mult)
-            eng.tensor_tensor(out=x3[:, s, 256:512], in0=x3[:, s, 256:512], in1=c3[:, s, :], op=ALU.mult)
-            eng.tensor_tensor(out=cn3[:, s, :], in0=x3[:, s, 0:256], in1=x3[:, s, 256:512], op=ALU.add)
-            nc.scalar.activation(out=x3[:, s, 512:768], in_=cn3[:, s, :], func=ACT.Tanh)
-            eng.tensor_tensor(out=hn3[:, s, :], in0=x3[:, s, 768:1024], in1=x3[:, s, 512:768], op=ALU.mult)
-            lo = (q * GT + a0) * H
-            nc.sync.dma_start(out=oc_v[:, lo:lo + na * H], in_=cn_t[q][:, a0 * H:(a0 + na) * H])
-            nc.sync.dma_start(out=oh_v[:, lo:lo + na * H], in_=hn_t[q][:, a0 * H:(a0 + na) * H])
-
-        for j in range(2):
-            add_bias(j)
-            transposes(j)
-            quantise(j)
         for j in range(NPAIR):
-            if j + 2 < NPAIR:
-                load_rec(j + 2)
-                load_h(j + 2)
-                if j % 2 == 0:
-                    load_c(j // 2 + 1)
-                transposes(j + 2)
-                add_bias(j + 2)
-            project(j)
-            if j + 2 < NPAIR:
-                quantise(j + 2)
-            activate(j)
-            q = j // 2
-            if q < POOL_GROUPS:
-                if j % 2 == 1:
-                    cell(q, 0, GT, nc.gpsimd)
-            else:
-                cell(q, (j % 2) * 2, 1, nc.vector)
-                cell(q, (j % 2) * 2 + 1, 1, nc.vector)
+            jl = j + LOOK
+            if jl < NPAIR:
+                if jl > 5:
+                    load_rec(jl)
+                load_h(jl)
+                if jl % 2 == 0:
+                    load_c(jl // 2)
+            if j in store_at:
+                store(oh_v, hn_t, store_at[j][0], store_at[j][1])
+            jb = j + 2
+            has = jb < NPAIR
+            vb = has and jb not in POOL_BIAS_PAIRS
+            if j >= 2 and has:
+                transposes(jb, 0)
+                transposes(jb, 1)
+            for a in range(2):
+                for nh in range(2):
+                    project(j, a, nh)
+            if j < 2 and has:
+                transposes(jb, 0)
+                transposes(jb, 1)
+            if j > 0:
+                activate(2 * j - 1)
+            if has:
+                regroup(jb, 0)
+                regroup(jb, 1)
+            if j in tanh_at:
+                cell_tanh(tanh_at[j][0], tanh_at[j][1])
+                store(oc_v, cn_t, tanh_at[j][0], tanh_at[j][1])
+            if j in state_at:
+                cell_state(state_at[j][0], state_at[j][1], nc.gpsimd)
+            if j in tanh_at:
+                hidden(tanh_at[j][0], tanh_at[j][1], nc.gpsimd)
+            vc = j > 0 and (2 * j - 1) not in pool_tiles
+            add_proj(j, 0, 0)
+            if vb:
+                add_bias(jb, 0)
+            add_proj(j, 0, 1)
+            activate(2 * j)
+            if vc:
+                cell_state(2 * j - 2, 2, nc.vector)
+                cell_tanh(2 * j - 2, 2)
+                store(oc_v, cn_t, 2 * j - 2, 2)
+            add_proj(j, 1, 0)
+            if vb:
+                add_bias(jb, 1)
+            add_proj(j, 1, 1)
+            if has:
+                quantise(jb)
+            if vc:
+                hidden(2 * j - 2, 2, nc.vector)
+                store(oh_v, hn_t, 2 * j - 2, 2)
+
+        activate(NT - 1)
+        cell_state(NT - 2, 1, nc.vector)
+        cell_tanh(NT - 2, 1)
+        cell_state(NT - 1, 1, nc.vector)
+        cell_tanh(NT - 1, 1)
+        store(oc_v, cn_t, NT - 2, 2)
+        hidden(NT - 2, 1, nc.vector)
+        hidden(NT - 1, 1, nc.vector)
+        for j in range(NPAIR, NPAIR + TANH_LAG + STORE_LAG):
+            if j in store_at:
+                store(oh_v, hn_t, store_at[j][0], store_at[j][1])
+        store(oh_v, hn_t, NT - 2, 2)

@@ -20,12 +20,9 @@ N = 1024
 H = 256
 NT = B // P
 GT = 4
+NG = NT // GT
 NPAIR = NT // 2
-LOOK = 4
-POOL_BIAS_PAIRS = (3, 4, 5)
-POOL_UNITS = ((0, 4), (4, 4), (8, 4), (12, 4), (16, 4), (20, 4), (24, 2))
-TANH_LAG = 2
-STORE_LAG = 2
+POOL_GROUPS = 7
 
 
 def tile_yourlstm_pc_t_kernel(tc, h_below, gates_rec, c, w_ih, b_ih, b_hh, out_0, out_1):
@@ -40,7 +37,7 @@ def tile_yourlstm_pc_t_kernel(tc, h_below, gates_rec, c, w_ih, b_ih, b_hh, out_0
     with ExitStack() as ctx:
         ctx.enter_context(tc.manual_schedule())
         const = ctx.enter_context(tc.tile_pool(name="const", bufs=1))
-        loads = ctx.enter_context(tc.tile_pool(name="loads", bufs=3))
+        loads = ctx.enter_context(tc.tile_pool(name="loads", bufs=6))
         work = ctx.enter_context(tc.tile_pool(name="work", bufs=3))
         psum = ctx.enter_context(tc.psum_pool(name="psum", bufs=1))
 
@@ -51,28 +48,26 @@ def tile_yourlstm_pc_t_kernel(tc, h_below, gates_rec, c, w_ih, b_ih, b_hh, out_0
         cn_t = {}
         hn_t = {}
         tp_t = {}
+        pre_t = {}
         gq_t = {}
         hc_t = {}
         hs_t = {}
         acc_t = {}
 
         def load_rec(j):
-            q = j // 2
-            if q not in r_t:
-                r_t[q] = loads.tile([P, GT * N], BF16, tag="rec", name="rec_sb")
-            lo = (j % 2) * 2 * N
-            nc.sync.dma_start(out=r_t[q][:, lo:lo + 2 * N], in_=r_v[:, j * 2 * N:(j + 1) * 2 * N])
+            if j < NPAIR:
+                r_t[j] = loads.tile([P, 2 * N], BF16, tag="rec", name="rec_sb")
+                nc.sync.dma_start(out=r_t[j][:], in_=r_v[:, j * 2 * N:(j + 1) * 2 * N])
 
         def load_h(j):
-            q = j // 2
-            if q not in h_t:
-                h_t[q] = loads.tile([P, GT * K], BF16, tag="h", name="h_sb")
-            lo = (j % 2) * 2 * K
-            nc.sync.dma_start(out=h_t[q][:, lo:lo + 2 * K], in_=h_v[:, j * 2 * K:(j + 1) * 2 * K])
+            if j < NPAIR:
+                h_t[j] = loads.tile([P, 2 * K], BF16, tag="h", name="h_sb")
+                nc.sync.dma_start(out=h_t[j][:], in_=h_v[:, j * 2 * K:(j + 1) * 2 * K])
 
         def load_c(q):
-            c_t[q] = loads.tile([P, GT * H], BF16, tag="c", bufs=4, name="c_sb")
-            nc.sync.dma_start(out=c_t[q][:], in_=c_v[:, q * GT * H:(q + 1) * GT * H])
+            if q < NG:
+                c_t[q] = loads.tile([P, GT * H], BF16, tag="c", bufs=4, name="c_sb")
+                nc.sync.dma_start(out=c_t[q][:], in_=c_v[:, q * GT * H:(q + 1) * GT * H])
 
         w_sb = const.tile([P, 8 * K], BF16, name="w_sb")
         w_sb3 = w_sb[:].rearrange("p (a k) -> p a k", a=8)
@@ -82,11 +77,13 @@ def tile_yourlstm_pc_t_kernel(tc, h_below, gates_rec, c, w_ih, b_ih, b_hh, out_0
 
         def x3(q):
             if q not in x_t:
-                x_t[q] = work.tile([P, GT * N], F32, tag="x", bufs=5, name="x_sb")
+                x_t[q] = work.tile([P, GT * N], F32, tag="x", bufs=4, name="x_sb")
             return x_t[q][:].rearrange("p (a n) -> p a n", a=GT)
 
         ident = const.tile([P, P], F32, name="ident")
         make_identity(nc, ident[:])
+        identb = const.tile([P, P], BF16, name="identb")
+        make_identity(nc, identb[:])
         ones = const.tile([P, P], BF16, name="ones")
         nc.vector.memset(ones[:], 1.0)
         brow = const.tile([P, N], BF16, name="brow")
@@ -98,84 +95,82 @@ def tile_yourlstm_pc_t_kernel(tc, h_below, gates_rec, c, w_ih, b_ih, b_hh, out_0
         nc.scalar.activation(out=warm[:], in_=warm[:], func=ACT.Sigmoid)
 
         load_rec(0)
-        load_w(0)
-        load_w(1)
-        load_rec(3)
-        load_w(2)
-        load_w(3)
+        for i in range(4):
+            load_w(i)
         load_h(0)
         load_rec(1)
         load_h(1)
         load_rec(2)
-        load_rec(4)
         load_h(2)
-        load_c(0)
         load_h(3)
-        load_rec(5)
+        load_c(0)
+        load_rec(3)
+        load_h(4)
+        load_h(5)
         load_c(1)
 
         bias_ps = [psum.tile([P, 512], F32, name="bias%d" % i) for i in range(2)]
-        bias_sb = const.tile([P, N], F32, name="bias_sb")
         for i in range(2):
             nc.tensor.matmul(bias_ps[i][:], lhsT=ones[:], rhs=brow[:, 512 * i:512 * (i + 1)], start=True, stop=True)
-        for i in range(2):
-            nc.scalar.copy(out=bias_sb[:, 512 * i:512 * (i + 1)], in_=bias_ps[i][:])
 
-        def add_bias(j, i):
-            q = j // 2
-            r3 = r_t[q][:].rearrange("p (a n) -> p a n", a=GT)
-            a0 = (j % 2) * 2
+        def add_bias(j, i, a0, na):
+            r3 = r_t[j][:].rearrange("p (a n) -> p a n", a=2)
+            g0 = (j % 2) * 2 + a0
             nc.vector.tensor_tensor(
-                out=x3(q)[:, a0:a0 + 2, 512 * i:512 * (i + 1)],
-                in0=bias_ps[i][:].unsqueeze(1).to_broadcast([P, 2, 512]),
-                in1=r3[:, a0:a0 + 2, 512 * i:512 * (i + 1)],
+                out=x3(j // 2)[:, g0:g0 + na, 512 * i:512 * (i + 1)],
+                in0=bias_ps[i][:].unsqueeze(1).to_broadcast([P, na, 512]),
+                in1=r3[:, a0:a0 + na, 512 * i:512 * (i + 1)],
                 op=ALU.add,
             )
 
-        def add_bias_pool(j):
-            q = j // 2
-            r3 = r_t[q][:].rearrange("p (a n) -> p a n", a=GT)
-            a0 = (j % 2) * 2
-            nc.gpsimd.tensor_tensor(
-                out=x3(q)[:, a0:a0 + 2, :],
-                in0=r3[:, a0:a0 + 2, :],
-                in1=bias_sb[:].unsqueeze(1).to_broadcast([P, 2, N]),
-                op=ALU.add,
-            )
+        def bias_matmul(j, a):
+            pre = psum.tile([P, 512], F32, tag="tp", bufs=2, name="pre")
+            pre_t[(j, a)] = pre
+            nc.tensor.matmul(pre[:], lhsT=identb[:], rhs=r_t[j][:, a * N + 512:(a + 1) * N], start=True, stop=False)
+            nc.tensor.matmul(pre[:], lhsT=ones[:], rhs=brow[:, 512:1024], start=False, stop=True)
+
+        def bias_copy(j, a):
+            nc.scalar.copy(out=x3(j // 2)[:, (j % 2) * 2 + a, 512:1024], in_=pre_t[(j, a)][:])
 
         def transposes(j, a):
-            words = h_t[j // 2][:].bitcast(F32)
-            tl = (j % 2) * 2 + a
+            words = h_t[j][:].bitcast(F32)
             tp = psum.tile([P, 512], F32, tag="tp", bufs=2, name="tp")
             tp_t[(j, a)] = tp
             for jj in range(4):
                 nc.tensor.transpose(
                     tp[:, P * jj:P * (jj + 1)],
-                    words[:, 512 * tl + P * jj:512 * tl + P * (jj + 1)],
+                    words[:, 512 * a + P * jj:512 * a + P * (jj + 1)],
                     ident[:],
                 )
 
         def regroup(j, a):
-            if a == 0:
-                gq_t[j] = work.tile([P, 2 * K], BF16, tag="gq", name="gq", align_bytes=64)
-            gq_w = gq_t[j][:].bitcast(F32).rearrange("p (a g r u) -> p a g r u", a=2, g=2, u=2)
-            nc.scalar.copy(out=gq_w[:, a], in_=tp_t[(j, a)][:].rearrange("p (g u r) -> p g r u", g=2, u=2))
+            q = j // 2
+            if q not in gq_t:
+                gq_t[q] = work.tile([P, GT * K], BF16, tag="gq", bufs=2, name="gq", align_bytes=64)
+            gq_w = gq_t[q][:].bitcast(F32).rearrange("p (t g r u) -> p t g r u", t=GT, g=2, u=2)
+            nc.scalar.copy(out=gq_w[:, (j % 2) * 2 + a], in_=tp_t[(j, a)][:].rearrange("p (g u r) -> p g r u", g=2, u=2))
 
-        def quantise(j):
-            hc_t[j] = work.tile([P, 512], U32, tag="hc", name="hc", align_bytes=64)
-            hs_t[j] = work.tile([P, 512], U8, tag="hs", name="hs", align_bytes=64)
-            nc.vector.quantize_mx(out=hc_t[j][:].bitcast(FP8X4), scales=hs_t[j][:], in_=gq_t[j][:])
+        def quantise(q, lo, n):
+            if q not in hc_t:
+                hc_t[q] = work.tile([P, GT * 256], U32, tag="hc", name="hc", align_bytes=64)
+                hs_t[q] = work.tile([P, GT * 256], U8, tag="hs", name="hs", align_bytes=64)
+            nc.vector.quantize_mx(
+                out=hc_t[q][:, lo * 256:(lo + n) * 256].bitcast(FP8X4),
+                scales=hs_t[q][:, lo * 256:(lo + n) * 256],
+                in_=gq_t[q][:, lo * K:(lo + n) * K],
+            )
 
         def project(j, a, nh):
             acc = psum.tile([P, 512], F32, tag="acc", bufs=4, name="acc")
             acc_t[(j, a, nh)] = acc
+            q = j // 2
             for g in range(2):
-                lo = (a * 2 + g) * P
+                lo = (((j % 2) * 2 + a) * 2 + g) * P
                 wlo = g * N + nh * 512
                 nc.tensor.matmul_mx(
                     out=acc[:],
-                    lhsT=hc_t[j][:, lo:lo + P].bitcast(FP8X4),
-                    lhsT_scale=hs_t[j][:, lo:lo + P],
+                    lhsT=hc_t[q][:, lo:lo + P].bitcast(FP8X4),
+                    lhsT_scale=hs_t[q][:, lo:lo + P],
                     rhs=wc[:, wlo:wlo + 512].bitcast(FP8X4),
                     rhs_scale=ws[:, wlo:wlo + 512],
                     start=(g == 0),
@@ -183,8 +178,7 @@ def tile_yourlstm_pc_t_kernel(tc, h_below, gates_rec, c, w_ih, b_ih, b_hh, out_0
                 )
 
         def add_proj(j, a, nh):
-            tl = (j % 2) * 2 + a
-            dst = x3(j // 2)[:, tl, 512 * nh:512 * (nh + 1)]
+            dst = x3(j // 2)[:, (j % 2) * 2 + a, 512 * nh:512 * (nh + 1)]
             nc.vector.tensor_tensor(out=dst, in0=acc_t[(j, a, nh)][:], in1=dst, op=ALU.add)
 
         def activate(t):
@@ -212,18 +206,17 @@ def tile_yourlstm_pc_t_kernel(tc, h_below, gates_rec, c, w_ih, b_ih, b_hh, out_0
             s = slice(t0 % GT, t0 % GT + nt)
             nc.scalar.activation(out=x3(q)[:, s, 512:768], in_=out3(cn_t, q, "cn")[:, s, :], func=ACT.Tanh)
 
-        def hidden(t0, nt, eng):
+        def hidden(t0, nt):
             q = t0 // GT
             s = slice(t0 % GT, t0 % GT + nt)
             x = x3(q)
-            eng.tensor_tensor(out=out3(hn_t, q, "hn")[:, s, :], in0=x[:, s, 768:1024], in1=x[:, s, 512:768], op=ALU.mult)
+            nc.vector.tensor_tensor(out=out3(hn_t, q, "hn")[:, s, :], in0=x[:, s, 768:1024], in1=x[:, s, 512:768], op=ALU.mult)
 
-        def store(dram, tiles, t0, nt):
-            lo = (t0 % GT) * H
-            nc.sync.dma_start(out=dram[:, t0 * H:(t0 + nt) * H], in_=tiles[t0 // GT][:, lo:lo + nt * H])
+        def store(dram, tiles, q):
+            nc.sync.dma_start(out=dram[:, q * GT * H:(q + 1) * GT * H], in_=tiles[q][:])
 
-        add_bias(0, 0)
-        add_bias(0, 1)
+        add_bias(0, 0, 0, 2)
+        add_bias(0, 1, 0, 2)
         w_words = w_sb[:].bitcast(F32)
         wq = const.tile([P, 2 * N * 4], BF16, name="wq", align_bytes=64)
         wq_w = wq[:].bitcast(F32).rearrange("p (g n u) -> p g n u", g=2, u=2)
@@ -251,94 +244,82 @@ def tile_yourlstm_pc_t_kernel(tc, h_below, gates_rec, c, w_ih, b_ih, b_hh, out_0
                         scales=ws[:, lo:lo + 512],
                         in_=wq[:, lo * 4:(lo + 512) * 4],
                     )
-        for j in POOL_BIAS_PAIRS:
-            add_bias_pool(j)
         for a in range(2):
             transposes(0, a)
             regroup(0, a)
-        quantise(0)
-        add_bias(1, 0)
-        add_bias(1, 1)
+        quantise(0, 0, 2)
+        add_bias(1, 0, 0, 2)
+        add_bias(1, 1, 0, 2)
         for a in range(2):
             transposes(1, a)
             regroup(1, a)
-        quantise(1)
-
-        state_at = {}
-        tanh_at = {}
-        store_at = {}
-        pool_tiles = set()
-        for u in POOL_UNITS:
-            step = (u[0] + u[1]) // 2
-            state_at[step] = u
-            tanh_at[step + TANH_LAG] = u
-            store_at[step + TANH_LAG + STORE_LAG] = u
-            for t in range(u[0], u[0] + u[1]):
-                pool_tiles.add(t)
+        quantise(0, 2, 2)
 
         for j in range(NPAIR):
-            jl = j + LOOK
-            if jl < NPAIR:
-                if jl > 5:
-                    load_rec(jl)
-                load_h(jl)
-                if jl % 2 == 0:
-                    load_c(jl // 2)
-            if j in store_at:
-                store(oh_v, hn_t, store_at[j][0], store_at[j][1])
+            q = j // 2
+            odd = j % 2 == 1
+            load_rec(j + 4)
+            if not odd:
+                load_c(q + 2)
+            load_h(j + 6)
             jb = j + 2
             has = jb < NPAIR
-            vb = has and jb not in POOL_BIAS_PAIRS
-            if j >= 2 and has:
-                transposes(jb, 0)
-                transposes(jb, 1)
+            by_pe = []
+            if has:
+                by_pe = [1] if jb % 2 == 0 else [0, 1]
+            if j == 0:
+                prep = [2, 3]
+            elif j == 1:
+                prep = [4, 5]
+            else:
+                prep = [j + 4] if j + 4 < NPAIR else []
+            for p in prep:
+                transposes(p, 0)
+                transposes(p, 1)
+            for a in by_pe:
+                bias_matmul(jb, a)
             for a in range(2):
                 for nh in range(2):
                     project(j, a, nh)
-            if j < 2 and has:
-                transposes(jb, 0)
-                transposes(jb, 1)
             if j > 0:
                 activate(2 * j - 1)
-            if has:
-                regroup(jb, 0)
-                regroup(jb, 1)
-            if j in tanh_at:
-                cell_tanh(tanh_at[j][0], tanh_at[j][1])
-                store(oc_v, cn_t, tanh_at[j][0], tanh_at[j][1])
-            if j in state_at:
-                cell_state(state_at[j][0], state_at[j][1], nc.gpsimd)
-            if j in tanh_at:
-                hidden(tanh_at[j][0], tanh_at[j][1], nc.gpsimd)
-            vc = j > 0 and (2 * j - 1) not in pool_tiles
+            if not odd and 1 <= q <= POOL_GROUPS:
+                cell_state(GT * (q - 1), GT, nc.gpsimd)
+            for p in prep:
+                regroup(p, 0)
+                regroup(p, 1)
+            for a in by_pe:
+                bias_copy(jb, a)
             add_proj(j, 0, 0)
-            if vb:
-                add_bias(jb, 0)
+            if has:
+                add_bias(jb, 0, 0, 2)
             add_proj(j, 0, 1)
             activate(2 * j)
-            if vc:
-                cell_state(2 * j - 2, 2, nc.vector)
-                cell_tanh(2 * j - 2, 2)
-                store(oc_v, cn_t, 2 * j - 2, 2)
+            if not odd and q >= 2:
+                cell_tanh(GT * (q - 2), GT)
+                store(oc_v, cn_t, q - 2)
             add_proj(j, 1, 0)
-            if vb:
-                add_bias(jb, 1)
+            if has and len(by_pe) == 1:
+                add_bias(jb, 1, 0, 1)
             add_proj(j, 1, 1)
-            if has:
-                quantise(jb)
-            if vc:
-                hidden(2 * j - 2, 2, nc.vector)
-                store(oh_v, hn_t, 2 * j - 2, 2)
+            if j == 0:
+                quantise(1, 0, GT)
+            if odd:
+                if q >= 2:
+                    hidden(GT * (q - 2), GT)
+                    store(oh_v, hn_t, q - 2)
+                if q + 2 < NG:
+                    quantise(q + 2, 0, GT)
 
         activate(NT - 1)
-        cell_state(NT - 2, 1, nc.vector)
-        cell_tanh(NT - 2, 1)
-        cell_state(NT - 1, 1, nc.vector)
-        cell_tanh(NT - 1, 1)
-        store(oc_v, cn_t, NT - 2, 2)
-        hidden(NT - 2, 1, nc.vector)
-        hidden(NT - 1, 1, nc.vector)
-        for j in range(NPAIR, NPAIR + TANH_LAG + STORE_LAG):
-            if j in store_at:
-                store(oh_v, hn_t, store_at[j][0], store_at[j][1])
-        store(oh_v, hn_t, NT - 2, 2)
+        cell_tanh(GT * 6, GT)
+        store(oc_v, cn_t, 6)
+        cell_state(GT * 7, 2, nc.vector)
+        cell_tanh(GT * 7, 2)
+        cell_state(GT * 7 + 2, 2, nc.vector)
+        cell_tanh(GT * 7 + 2, 2)
+        store(oc_v, cn_t, 7)
+        hidden(GT * 6, GT)
+        store(oh_v, hn_t, 6)
+        hidden(GT * 7, GT)
+        store(oh_v, hn_t, 7)

@@ -212,8 +212,9 @@ def tile_yourlstm_pc_t_kernel(tc, h_below, gates_rec, c, w_ih, b_ih, b_hh, out_0
             x = x3(q)
             nc.vector.tensor_tensor(out=out3(hn_t, q, "hn")[:, s, :], in0=x[:, s, 768:1024], in1=x[:, s, 512:768], op=ALU.mult)
 
-        def store(dram, tiles, q):
-            nc.sync.dma_start(out=dram[:, q * GT * H:(q + 1) * GT * H], in_=tiles[q][:])
+        def store(dram, tiles, t0, nt):
+            lo = (t0 % GT) * H
+            nc.sync.dma_start(out=dram[:, t0 * H:(t0 + nt) * H], in_=tiles[t0 // GT][:, lo:lo + nt * H])
 
         add_bias(0, 0, 0, 2)
         add_bias(0, 1, 0, 2)
@@ -248,11 +249,14 @@ def tile_yourlstm_pc_t_kernel(tc, h_below, gates_rec, c, w_ih, b_ih, b_hh, out_0
             transposes(0, a)
             regroup(0, a)
         quantise(0, 0, 2)
-        add_bias(1, 0, 0, 2)
-        add_bias(1, 1, 0, 2)
         for a in range(2):
             transposes(1, a)
             regroup(1, a)
+        for a in range(2):
+            for nh in range(2):
+                project(0, a, nh)
+        add_bias(1, 0, 0, 2)
+        add_bias(1, 1, 0, 2)
         quantise(0, 2, 2)
 
         for j in range(NPAIR):
@@ -264,6 +268,7 @@ def tile_yourlstm_pc_t_kernel(tc, h_below, gates_rec, c, w_ih, b_ih, b_hh, out_0
             load_h(j + 6)
             jb = j + 2
             has = jb < NPAIR
+            more = j + 1 < NPAIR
             by_pe = []
             if has:
                 by_pe = [1] if jb % 2 == 0 else [0, 1]
@@ -276,50 +281,57 @@ def tile_yourlstm_pc_t_kernel(tc, h_below, gates_rec, c, w_ih, b_ih, b_hh, out_0
             for p in prep:
                 transposes(p, 0)
                 transposes(p, 1)
-            for a in by_pe:
-                bias_matmul(jb, a)
-            for a in range(2):
-                for nh in range(2):
-                    project(j, a, nh)
+                regroup(p, 0)
+                regroup(p, 1)
+            add_proj(j, 0, 0)
+            if more:
+                project(j + 1, 0, 0)
+            if has:
+                bias_matmul(jb, by_pe[0])
             if j > 0:
                 activate(2 * j - 1)
             if not odd and 1 <= q <= POOL_GROUPS:
                 cell_state(GT * (q - 1), GT, nc.gpsimd)
-            for p in prep:
-                regroup(p, 0)
-                regroup(p, 1)
-            for a in by_pe:
-                bias_copy(jb, a)
-            add_proj(j, 0, 0)
             if has:
+                bias_copy(jb, by_pe[0])
                 add_bias(jb, 0, 0, 2)
             add_proj(j, 0, 1)
+            if more:
+                project(j + 1, 0, 1)
+            if len(by_pe) == 2:
+                bias_matmul(jb, by_pe[1])
+                bias_copy(jb, by_pe[1])
             activate(2 * j)
             if not odd and q >= 2:
                 cell_tanh(GT * (q - 2), GT)
-                store(oc_v, cn_t, q - 2)
+                store(oc_v, cn_t, GT * (q - 2), GT)
             add_proj(j, 1, 0)
-            if has and len(by_pe) == 1:
+            if more:
+                project(j + 1, 1, 0)
+            if len(by_pe) == 1:
                 add_bias(jb, 1, 0, 1)
             add_proj(j, 1, 1)
+            if more:
+                project(j + 1, 1, 1)
             if j == 0:
                 quantise(1, 0, GT)
             if odd:
                 if q >= 2:
                     hidden(GT * (q - 2), GT)
-                    store(oh_v, hn_t, q - 2)
+                    store(oh_v, hn_t, GT * (q - 2), GT)
                 if q + 2 < NG:
                     quantise(q + 2, 0, GT)
 
+        cell_state(NT - 4, 2, nc.vector)
         activate(NT - 1)
-        cell_tanh(GT * 6, GT)
-        store(oc_v, cn_t, 6)
-        cell_state(GT * 7, 2, nc.vector)
-        cell_tanh(GT * 7, 2)
-        cell_state(GT * 7 + 2, 2, nc.vector)
-        cell_tanh(GT * 7 + 2, 2)
-        store(oc_v, cn_t, 7)
-        hidden(GT * 6, GT)
-        store(oh_v, hn_t, 6)
-        hidden(GT * 7, GT)
-        store(oh_v, hn_t, 7)
+        cell_tanh(NT - 8, GT)
+        store(oc_v, cn_t, NT - 8, GT)
+        cell_tanh(NT - 4, 2)
+        store(oc_v, cn_t, NT - 4, 2)
+        cell_state(NT - 2, 2, nc.vector)
+        cell_tanh(NT - 2, 2)
+        store(oc_v, cn_t, NT - 2, 2)
+        hidden(NT - 8, GT)
+        store(oh_v, hn_t, NT - 8, GT)
+        hidden(NT - 4, GT)
+        store(oh_v, hn_t, NT - 4, GT)

@@ -22,7 +22,7 @@ NT = B // P
 GT = 4
 NG = NT // GT
 NPAIR = NT // 2
-POOL_GROUPS = 7
+POOL_GROUPS = 6
 
 
 def tile_yourlstm_pc_t_kernel(tc, h_below, gates_rec, c, w_ih, b_ih, b_hh, out_0, out_1):
@@ -98,8 +98,8 @@ def tile_yourlstm_pc_t_kernel(tc, h_below, gates_rec, c, w_ih, b_ih, b_hh, out_0
         for i in range(4):
             load_w(i)
         load_h(0)
-        load_rec(1)
         load_h(1)
+        load_rec(1)
         load_rec(2)
         load_h(2)
         load_h(3)
@@ -315,23 +315,30 @@ def tile_yourlstm_pc_t_kernel(tc, h_below, gates_rec, c, w_ih, b_ih, b_hh, out_0
                 project(j + 1, 1, 1)
             if j == 0:
                 quantise(1, 0, GT)
-            if odd:
-                if q >= 2:
-                    hidden(GT * (q - 2), GT)
-                    store(oh_v, hn_t, GT * (q - 2), GT)
-                if q + 2 < NG:
-                    quantise(q + 2, 0, GT)
+            if odd and 2 <= q <= 5:
+                hidden(GT * (q - 2), GT)
+                store(oh_v, hn_t, GT * (q - 2), GT)
+            if j == NPAIR - 2:
+                hidden(GT * 4, GT)
+                store(oh_v, hn_t, GT * 4, GT)
+            if odd and q + 2 < NG:
+                quantise(q + 2, 0, GT)
 
-        cell_state(NT - 4, 2, nc.vector)
+        cell_state(GT * 6, GT, nc.vector)
         activate(NT - 1)
-        cell_tanh(NT - 8, GT)
-        store(oc_v, cn_t, NT - 8, GT)
+        cell_tanh(GT * 6, GT)
+        store(oc_v, cn_t, GT * 6, GT)
+        hidden(GT * 5, GT)
+        store(oh_v, hn_t, GT * 5, GT)
+        cell_state(NT - 4, 2, nc.vector)
         cell_tanh(NT - 4, 2)
         store(oc_v, cn_t, NT - 4, 2)
+        hidden(GT * 6, GT)
+        store(oh_v, hn_t, GT * 6, GT)
         cell_state(NT - 2, 2, nc.vector)
         cell_tanh(NT - 2, 2)
         store(oc_v, cn_t, NT - 2, 2)
-        hidden(NT - 8, GT)
-        store(oh_v, hn_t, NT - 8, GT)
-        hidden(NT - 4, GT)
-        store(oh_v, hn_t, NT - 4, GT)
+        hidden(NT - 4, 2)
+        store(oh_v, hn_t, NT - 4, 2)
+        hidden(NT - 2, 2)
+        store(oh_v, hn_t, NT - 2, 2)

@@ -271,7 +271,7 @@ def tile_yourlstm_pc_t_kernel(tc, h_below, gates_rec, c, w_ih, b_ih, b_hh, out_0
             more = j + 1 < NPAIR
             by_pe = []
             if has:
-                by_pe = [1] if jb % 2 == 0 else [0, 1]
+                by_pe = [0, 1] if (jb % 2 == 1 or jb % 4 == 0) else [1]
             if j == 0:
                 prep = [2, 3]
             elif j == 1:

@@ -35,7 +35,6 @@ def tile_yourlstm_pc_t_kernel(tc, h_below, gates_rec, c, w_ih, b_ih, b_hh, out_0
     w_v = w_ih.rearrange("(a p) k -> p a k", p=P)
 
     with ExitStack() as ctx:
-        ctx.enter_context(tc.manual_schedule())
         const = ctx.enter_context(tc.tile_pool(name="const", bufs=1))
         loads = ctx.enter_context(tc.tile_pool(name="loads", bufs=6))
         work = ctx.enter_context(tc.tile_pool(name="work", bufs=3))
@@ -271,7 +270,7 @@ def tile_yourlstm_pc_t_kernel(tc, h_below, gates_rec, c, w_ih, b_ih, b_hh, out_0
             more = j + 1 < NPAIR
             by_pe = []
             if has:
-                by_pe = [0, 1] if (jb % 2 == 1 or jb % 4 == 0) else [1]
+                by_pe = [1] if jb % 2 == 0 else [0, 1]
             if j == 0:
                 prep = [2, 3]
             elif j == 1:

from contextlib import ExitStack

import concourse.mybir as mybir
from concourse.masks import make_identity

FLOPS = 2 * 4096 * 1024 * 1024

F32 = mybir.dt.float32
BF16 = mybir.dt.bfloat16
U32 = mybir.dt.uint32
U8 = mybir.dt.uint8
FP8X4 = mybir.dt.float8_e4m3fn_x4
ACT = mybir.ActivationFunctionType
ALU = mybir.AluOpType

P = 128
B = 4096
K = 1024
N = 1024
H = 256
NT = B // P
GT = 4
NG = NT // GT
NPAIR = NT // 2
POOL_GROUPS = 6


def tile_yourlstm_pc_t_kernel(tc, h_below, gates_rec, c, w_ih, b_ih, b_hh, out_0, out_1):
    nc = tc.nc
    h_v = h_below.rearrange("(p t) k -> p (t k)", t=NT)
    r_v = gates_rec.rearrange("(p t) n -> p (t n)", t=NT)
    c_v = c.rearrange("(p t) n -> p (t n)", t=NT)
    oh_v = out_0.rearrange("(p t) n -> p (t n)", t=NT)
    oc_v = out_1.rearrange("(p t) n -> p (t n)", t=NT)
    w_v = w_ih.rearrange("(a p) k -> p a k", p=P)

    with ExitStack() as ctx:
        const = ctx.enter_context(tc.tile_pool(name="const", bufs=1))
        loads = ctx.enter_context(tc.tile_pool(name="loads", bufs=6))
        work = ctx.enter_context(tc.tile_pool(name="work", bufs=3))
        psum = ctx.enter_context(tc.psum_pool(name="psum", bufs=1))

        h_t = {}
        r_t = {}
        c_t = {}
        x_t = {}
        cn_t = {}
        hn_t = {}
        tp_t = {}
        pre_t = {}
        gq_t = {}
        hc_t = {}
        hs_t = {}
        acc_t = {}

        def load_rec(j):
            if j < NPAIR:
                r_t[j] = loads.tile([P, 2 * N], BF16, tag="rec", name="rec_sb")
                nc.sync.dma_start(out=r_t[j][:], in_=r_v[:, j * 2 * N:(j + 1) * 2 * N])

        def load_h(j):
            if j < NPAIR:
                h_t[j] = loads.tile([P, 2 * K], BF16, tag="h", name="h_sb")
                nc.sync.dma_start(out=h_t[j][:], in_=h_v[:, j * 2 * K:(j + 1) * 2 * K])

        def load_c(q):
            if q < NG:
                c_t[q] = loads.tile([P, GT * H], BF16, tag="c", bufs=4, name="c_sb")
                nc.sync.dma_start(out=c_t[q][:], in_=c_v[:, q * GT * H:(q + 1) * GT * H])

        w_sb = const.tile([P, 8 * K], BF16, name="w_sb")
        w_sb3 = w_sb[:].rearrange("p (a k) -> p a k", a=8)

        def load_w(i):
            nc.sync.dma_start(out=w_sb3[:, 2 * i:2 * i + 2, :], in_=w_v[:, 2 * i:2 * i + 2, :])

        def x3(q):
            if q not in x_t:
                x_t[q] = work.tile([P, GT * N], F32, tag="x", bufs=4, name="x_sb")
            return x_t[q][:].rearrange("p (a n) -> p a n", a=GT)

        ident = const.tile([P, P], F32, name="ident")
        make_identity(nc, ident[:])
        identb = const.tile([P, P], BF16, name="identb")
        make_identity(nc, identb[:])
        ones = const.tile([P, P], BF16, name="ones")
        nc.vector.memset(ones[:], 1.0)
        brow = const.tile([P, N], BF16, name="brow")
        nc.vector.memset(brow[:], 0.0)
        nc.sync.dma_start(out=brow[0:1, :], in_=b_ih.rearrange("(o n) -> o n", o=1))
        nc.sync.dma_start(out=brow[1:2, :], in_=b_hh.rearrange("(o n) -> o n", o=1))
        warm = const.tile([P, 1], F32, name="warm")
        nc.vector.memset(warm[:], 0.0)
        nc.scalar.activation(out=warm[:], in_=warm[:], func=ACT.Sigmoid)

        load_rec(0)
        for i in range(4):
            load_w(i)
        load_h(0)
        load_h(1)
        load_rec(1)
        load_rec(2)
        load_h(2)
        load_h(3)
        load_c(0)
        load_rec(3)
        load_h(4)
        load_h(5)
        load_c(1)

        bias_ps = [psum.tile([P, 512], F32, name="bias%d" % i) for i in range(2)]
        for i in range(2):
            nc.tensor.matmul(bias_ps[i][:], lhsT=ones[:], rhs=brow[:, 512 * i:512 * (i + 1)], start=True, stop=True)

        def add_bias(j, i, a0, na):
            r3 = r_t[j][:].rearrange("p (a n) -> p a n", a=2)
            g0 = (j % 2) * 2 + a0
            nc.vector.tensor_tensor(
                out=x3(j // 2)[:, g0:g0 + na, 512 * i:512 * (i + 1)],
                in0=bias_ps[i][:].unsqueeze(1).to_broadcast([P, na, 512]),
                in1=r3[:, a0:a0 + na, 512 * i:512 * (i + 1)],
                op=ALU.add,
            )

        def bias_matmul(j, a):
            pre = psum.tile([P, 512], F32, tag="tp", bufs=2, name="pre")
            pre_t[(j, a)] = pre
            nc.tensor.matmul(pre[:], lhsT=identb[:], rhs=r_t[j][:, a * N + 512:(a + 1) * N], start=True, stop=False)
            nc.tensor.matmul(pre[:], lhsT=ones[:], rhs=brow[:, 512:1024], start=False, stop=True)

        def bias_copy(j, a):
            nc.scalar.copy(out=x3(j // 2)[:, (j % 2) * 2 + a, 512:1024], in_=pre_t[(j, a)][:])

        def transposes(j, a):
            words = h_t[j][:].bitcast(F32)
            tp = psum.tile([P, 512], F32, tag="tp", bufs=2, name="tp")
            tp_t[(j, a)] = tp
            for jj in range(4):
                nc.tensor.transpose(
                    tp[:, P * jj:P * (jj + 1)],
                    words[:, 512 * a + P * jj:512 * a + P * (jj + 1)],
                    ident[:],
                )

        def regroup(j, a):
            q = j // 2
            if q not in gq_t:
                gq_t[q] = work.tile([P, GT * K], BF16, tag="gq", bufs=2, name="gq", align_bytes=64)
            gq_w = gq_t[q][:].bitcast(F32).rearrange("p (t g r u) -> p t g r u", t=GT, g=2, u=2)
            nc.scalar.copy(out=gq_w[:, (j % 2) * 2 + a], in_=tp_t[(j, a)][:].rearrange("p (g u r) -> p g r u", g=2, u=2))

        def quantise(q, lo, n):
            if q not in hc_t:
                hc_t[q] = work.tile([P, GT * 256], U32, tag="hc", name="hc", align_bytes=64)
                hs_t[q] = work.tile([P, GT * 256], U8, tag="hs", name="hs", align_bytes=64)
            nc.vector.quantize_mx(
                out=hc_t[q][:, lo * 256:(lo + n) * 256].bitcast(FP8X4),
                scales=hs_t[q][:, lo * 256:(lo + n) * 256],
                in_=gq_t[q][:, lo * K:(lo + n) * K],
            )

        def project(j, a, nh):
            acc = psum.tile([P, 512], F32, tag="acc", bufs=4, name="acc")
            acc_t[(j, a, nh)] = acc
            q = j // 2
            for g in range(2):
                lo = (((j % 2) * 2 + a) * 2 + g) * P
                wlo = g * N + nh * 512
                nc.tensor.matmul_mx(
                    out=acc[:],
                    lhsT=hc_t[q][:, lo:lo + P].bitcast(FP8X4),
                    lhsT_scale=hs_t[q][:, lo:lo + P],
                    rhs=wc[:, wlo:wlo + 512].bitcast(FP8X4),
                    rhs_scale=ws[:, wlo:wlo + 512],
                    start=(g == 0),
                    stop=(g == 1),
                )

        def add_proj(j, a, nh):
            dst = x3(j // 2)[:, (j % 2) * 2 + a, 512 * nh:512 * (nh + 1)]
            nc.vector.tensor_tensor(out=dst, in0=acc_t[(j, a, nh)][:], in1=dst, op=ALU.add)

        def activate(t):
            xt = x3(t // GT)[:, t % GT, :]
            nc.scalar.activation(out=xt[:, 0:512], in_=xt[:, 0:512], func=ACT.Sigmoid)
            nc.scalar.activation(out=xt[:, 512:768], in_=xt[:, 512:768], func=ACT.Tanh)
            nc.scalar.activation(out=xt[:, 768:1024], in_=xt[:, 768:1024], func=ACT.Sigmoid)

        def out3(tiles, q, tag):
            if q not in tiles:
                tiles[q] = work.tile([P, GT * H], F32, tag=tag, name=tag + "_sb")
            return tiles[q][:].rearrange("p (a n) -> p a n", a=GT)

        def cell_state(t0, nt, eng):
            q = t0 // GT
            s = slice(t0 % GT, t0 % GT + nt)
            x = x3(q)
            c3 = c_t[q][:].rearrange("p (a n) -> p a n", a=GT)
            eng.tensor_tensor(out=x[:, s, 0:256], in0=x[:, s, 0:256], in1=x[:, s, 512:768], op=ALU.mult)
            eng.tensor_tensor(out=x[:, s, 256:512], in0=x[:, s, 256:512], in1=c3[:, s, :], op=ALU.mult)
            eng.tensor_tensor(out=out3(cn_t, q, "cn")[:, s, :], in0=x[:, s, 0:256], in1=x[:, s, 256:512], op=ALU.add)

        def cell_tanh(t0, nt):
            q = t0 // GT
            s = slice(t0 % GT, t0 % GT + nt)
            nc.scalar.activation(out=x3(q)[:, s, 512:768], in_=out3(cn_t, q, "cn")[:, s, :], func=ACT.Tanh)

        def hidden(t0, nt):
            q = t0 // GT
            s = slice(t0 % GT, t0 % GT + nt)
            x = x3(q)
            nc.vector.tensor_tensor(out=out3(hn_t, q, "hn")[:, s, :], in0=x[:, s, 768:1024], in1=x[:, s, 512:768], op=ALU.mult)

        def store(dram, tiles, t0, nt):
            lo = (t0 % GT) * H
            nc.sync.dma_start(out=dram[:, t0 * H:(t0 + nt) * H], in_=tiles[t0 // GT][:, lo:lo + nt * H])

        add_bias(0, 0, 0, 2)
        add_bias(0, 1, 0, 2)
        w_words = w_sb[:].bitcast(F32)
        wq = const.tile([P, 2 * N * 4], BF16, name="wq", align_bytes=64)
        wq_w = wq[:].bitcast(F32).rearrange("p (g n u) -> p g n u", g=2, u=2)
        wc = const.tile([P, 2 * N], U32, name="wc", align_bytes=64)
        ws = const.tile([P, 2 * N], U8, name="ws", align_bytes=64)
        for a in range(8):
            wtp = psum.tile([P, 512], F32, tag="acc", bufs=4, name="wtp")
            for jj in range(4):
                nc.tensor.transpose(
                    wtp[:, P * jj:P * (jj + 1)],
                    w_words[:, 512 * a + P * jj:512 * a + P * (jj + 1)],
                    ident[:],
                )
            src = wtp[:].rearrange("p (g u r) -> p g r u", g=2, u=2)
            dst = wq_w[:, :, P * a:P * (a + 1), :]
            if a % 2 == 1:
                nc.vector.tensor_copy(out=dst, in_=src)
            else:
                nc.scalar.copy(out=dst, in_=src)
            if a % 4 == 3:
                for g in range(2):
                    lo = g * N + (a // 4) * 512
                    nc.vector.quantize_mx(
                        out=wc[:, lo:lo + 512].bitcast(FP8X4),
                        scales=ws[:, lo:lo + 512],
                        in_=wq[:, lo * 4:(lo + 512) * 4],
                    )
        for a in range(2):
            transposes(0, a)
            regroup(0, a)
        quantise(0, 0, 2)
        for a in range(2):
            transposes(1, a)
            regroup(1, a)
        for a in range(2):
            for nh in range(2):
                project(0, a, nh)
        add_bias(1, 0, 0, 2)
        add_bias(1, 1, 0, 2)
        quantise(0, 2, 2)

        for j in range(NPAIR):
            q = j // 2
            odd = j % 2 == 1
            load_rec(j + 4)
            if not odd:
                load_c(q + 2)
            load_h(j + 6)
            jb = j + 2
            has = jb < NPAIR
            more = j + 1 < NPAIR
            by_pe = []
            if has:
                by_pe = [1] if jb % 2 == 0 else [0, 1]
            if j == 0:
                prep = [2, 3]
            elif j == 1:
                prep = [4, 5]
            else:
                prep = [j + 4] if j + 4 < NPAIR else []
            for p in prep:
                transposes(p, 0)
                transposes(p, 1)
                regroup(p, 0)
                regroup(p, 1)
            add_proj(j, 0, 0)
            if more:
                project(j + 1, 0, 0)
            if has:
                bias_matmul(jb, by_pe[0])
            if j > 0:
                activate(2 * j - 1)
            if not odd and 1 <= q <= POOL_GROUPS:
                cell_state(GT * (q - 1), GT, nc.gpsimd)
            if has:
                bias_copy(jb, by_pe[0])
                add_bias(jb, 0, 0, 2)
            add_proj(j, 0, 1)
            if more:
                project(j + 1, 0, 1)
            if len(by_pe) == 2:
                bias_matmul(jb, by_pe[1])
                bias_copy(jb, by_pe[1])
            activate(2 * j)
            if not odd and q >= 2:
                cell_tanh(GT * (q - 2), GT)
                store(oc_v, cn_t, GT * (q - 2), GT)
            add_proj(j, 1, 0)
            if more:
                project(j + 1, 1, 0)
            if len(by_pe) == 1:
                add_bias(jb, 1, 0, 1)
            add_proj(j, 1, 1)
            if more:
                project(j + 1, 1, 1)
            if j == 0:
                quantise(1, 0, GT)
            if odd and 2 <= q <= 5:
                hidden(GT * (q - 2), GT)
                store(oh_v, hn_t, GT * (q - 2), GT)
            if j == NPAIR - 2:
                hidden(GT * 4, GT)
                store(oh_v, hn_t, GT * 4, GT)
            if odd and q + 2 < NG:
                quantise(q + 2, 0, GT)

        cell_state(GT * 6, GT, nc.vector)
        activate(NT - 1)
        cell_tanh(GT * 6, GT)
        store(oc_v, cn_t, GT * 6, GT)
        hidden(GT * 5, GT)
        store(oh_v, hn_t, GT * 5, GT)
        cell_state(NT - 4, 2, nc.vector)
        cell_tanh(NT - 4, 2)
        store(oc_v, cn_t, NT - 4, 2)
        hidden(GT * 6, GT)
        store(oh_v, hn_t, GT * 6, GT)
        cell_state(NT - 2, 2, nc.vector)
        cell_tanh(NT - 2, 2)
        store(oc_v, cn_t, NT - 2, 2)
        hidden(NT - 4, 2)
        store(oh_v, hn_t, NT - 4, 2)
        hidden(NT - 2, 2)
        store(oh_v, hn_t, NT - 2, 2)
